import numpy as np
import ml_dtypes


def mxq(x, axis, fmt="e4m3"):
    dtype, down = {"e4m3": (ml_dtypes.float8_e4m3fn, 7), "e5m2": (ml_dtypes.float8_e5m2, 14)}[fmt]
    v = np.moveaxis(np.asarray(x, np.float32).astype(ml_dtypes.bfloat16).astype(np.float64), axis, -1)
    blocks = v.reshape(v.shape[:-1] + (-1, 32))
    amax = np.abs(blocks).max(-1, keepdims=True)
    byte = np.maximum(np.where(amax > 0, np.frexp(amax)[1] - 1 + 127, 0) - down, 1)
    scale = np.exp2(byte - 127.0)
    codes = (blocks / scale).astype(np.float32).astype(dtype).astype(np.float64)
    return np.moveaxis((codes * scale).reshape(v.shape), -1, axis)


WIDE = False


def mx_kscale(k):
    if not WIDE:
        return np.ones(k)
    levels = np.array([10, -10, 5, -5, 0])
    if k % 512:
        return np.exp2(np.random.permutation(np.resize(levels, k // 32))).repeat(32)
    a = np.empty((k // 512, 16))
    for p in range(k // 512):
        a[p, :8] = np.random.permutation(np.resize(levels, 8))
        for g in range(8):
            far = levels[np.abs(levels - a[p, g]) >= 10]
            a[p, g + 8] = far[np.random.randint(len(far))]
    return np.exp2(a.ravel()).repeat(32)


BF16 = ml_dtypes.bfloat16


def bf(x):
    return np.asarray(x, np.float32).astype(BF16)


def f64(x):
    return np.asarray(x).astype(np.float64)


N, C, F, G = 512, 3, 1024, 1024
F2 = F + F
F3 = F2 + F


def silu(v):
    return v / (1.0 + np.exp(-v))


def draw0():
    s = mx_kscale(G)
    return {"h": bf(silu(1.4 * np.random.standard_normal((N, 1, G))) * s),
            "mu_W": bf(np.random.standard_normal((N, C, F))),
            "mu_VW": bf(np.sqrt(C) * np.random.standard_normal((N, 1, F))),
            "q": bf(np.random.standard_normal((N, 1, F))),
            "mu": bf(np.random.standard_normal((N, C, F))),
            "W2": bf(np.random.standard_normal((F3, G)) / np.sqrt(G) / s),
            "b2": bf(0.2 * np.random.standard_normal(F3))}


def core(h, mu_W, mu_VW, q, mu, W2, b2):
    x = (mxq(f64(h), 2, "e4m3") @ mxq(f64(W2), 1, "e4m3").T) + f64(b2)
    dq_intra = x[..., :F]
    dmu_intra = x[..., F:F2] * f64(mu_W)
    dqmu_intra = x[..., F2:] * f64(mu_VW)
    q_out = f64(q) + dq_intra + dqmu_intra
    mu_out = f64(mu) + dmu_intra
    return q_out, mu_out


def e4m3fn_bytes(y):
    return np.clip(np.asarray(y, np.float64), -448.0, 448.0).astype(np.float32).astype(ml_dtypes.float8_e4m3fn).view(np.uint8)


def e4m3fn_values(b):
    return np.asarray(b, np.uint8).view(ml_dtypes.float8_e4m3fn).astype(np.float64)


def setup_inputs():
    d = draw0()
    x0 = np.asarray(d['W2']).astype(np.float64)
    s = (np.max(np.abs(x0), axis=(0,), keepdims=True) / 448.0).astype(np.float32)
    out = {}
    for k, v in d.items():
        if k == 'W2':
            out['W2_bytes'] = e4m3fn_bytes(x0 / s.astype(np.float64))
            out['W2_scale'] = s
        else:
            out[k] = v
    return out


def reference(h, mu_W, mu_VW, q, mu, W2_bytes, W2_scale, b2):
    return core(h, mu_W, mu_VW, q, mu, e4m3fn_values(W2_bytes) * W2_scale.astype(np.float64), b2)

@@ -1,0 +1,399 @@
+from contextlib import ExitStack
+
+import concourse.mybir as mybir
+from concourse.masks import make_identity
+
+FLOPS = 2 * 512 * 3072 * 1024
+
+F32 = mybir.dt.float32
+BF16 = mybir.dt.bfloat16
+U32 = mybir.dt.uint32
+U8 = mybir.dt.uint8
+FP8 = mybir.dt.float8_e4m3fn
+FP8X4 = mybir.dt.float8_e4m3fn_x4
+ALU = mybir.AluOpType
+ACT = mybir.ActivationFunctionType
+
+P = 128
+CYC = [
+    [(2, 0), (2, 1)],
+    [(1, 0), (0, 0)],
+    [(1, 1), (0, 1)],
+    [(1, 2), (1, 3)],
+    [(2, 2), (0, 2)],
+    [(2, 3), (0, 3)],
+]
+IN_PSUM = (0, 1)
+MANUAL = True
+
+
+def tile_painnmixing_pb_kernel(tc, h, mu_W, mu_VW, q, mu, W2_bytes, W2_scale, b2, out_0, out_1):
+    nc = tc.nc
+    n_cyc = len(CYC)
+
+    with ExitStack() as ctx:
+        const = ctx.enter_context(tc.tile_pool(name="const", bufs=1))
+        inp = ctx.enter_context(tc.tile_pool(name="inp", bufs=1))
+        wbf_pool = ctx.enter_context(tc.tile_pool(name="wbfp", bufs=5))
+        grp_pool = ctx.enter_context(tc.tile_pool(name="grpp", bufs=3))
+        code_pool = ctx.enter_context(tc.tile_pool(name="codep", bufs=2))
+        xb_pool = ctx.enter_context(tc.tile_pool(name="xbp", bufs=6))
+        mo_pool = ctx.enter_context(tc.tile_pool(name="mop", bufs=4))
+        qo_pool = ctx.enter_context(tc.tile_pool(name="qop", bufs=6))
+        tt_pool = ctx.enter_context(tc.tile_pool(name="ttp", bufs=4))
+        pw = ctx.enter_context(tc.psum_pool(name="pw", bufs=3))
+        pm = ctx.enter_context(tc.psum_pool(name="pm", bufs=2))
+        px = ctx.enter_context(tc.psum_pool(name="px", bufs=3))
+        if MANUAL:
+            ctx.enter_context(tc.manual_schedule())
+
+        s4 = const.tile([P, 2, 4], F32, name="s4")
+        nc.sync.dma_start(out=s4[:], in_=W2_scale.rearrange("o (g p t) -> p (o g) t", g=2, p=P, t=4))
+        bt = const.tile([P, P], BF16, name="bt")
+        nc.vector.memset(bt[:], 0.0)
+        nc.scalar.dma_start(out=bt[0:24, :], in_=b2.rearrange("(j p) -> j p", p=P))
+
+        warm = const.tile([P, 1], F32, name="warm")
+        warm2 = const.tile([P, 1], F32, name="warm2")
+        nc.vector.memset(warm[:], 0.0)
+        nc.scalar.activation(out=warm2[:], in_=warm[:], func=ACT.Identity)
+
+        ident_f = const.tile([P, P], F32, name="ident_f")
+        make_identity(nc, ident_f[:])
+        ident_b = const.tile([P, P], BF16, name="ident_b")
+        make_identity(nc, ident_b[:])
+
+        zer = const.tile([P, 512], BF16, name="zer")
+        nc.vector.memset(zer[:], 0.0)
+
+        def dummy(k):
+            for r in range(k):
+                dm = pm.tile([P, 512], F32, name="dm", tag="mx")
+                nc.tensor.matmul(out=dm[:], lhsT=ident_b[:], rhs=zer[:], start=True, stop=True)
+
+        dummy(4)
+        w2v = W2_bytes.rearrange("(n p) k -> p n k", p=P)
+        wb8 = {}
+
+        def load_w(c, pr):
+            s, i = CYC[c][pr]
+            t = inp.tile([P, 2, 1024], U8, name="wb8_%d_%d" % (c, pr))
+            rt = s * 8 + 2 * i
+            nc.sync.dma_start(out=t[:], in_=w2v[:, rt:rt + 2, :])
+            wb8[(c, pr)] = t
+
+        h_sb = inp.tile([P, 4, 1024], BF16, name="h_sb")
+        hv = h.rearrange("(a p) o k -> p a (o k)", p=P)
+        muW_sb = inp.tile([P, 4, 3, 1024], BF16, name="muW_sb")
+        mu_sb = inp.tile([P, 4, 3, 1024], BF16, name="mu_sb")
+        muVW_sb = inp.tile([P, 4, 1024], BF16, name="muVW_sb")
+        q_sb = inp.tile([P, 4, 1024], BF16, name="q_sb")
+
+        def load_muw(a):
+            nc.sync.dma_start(out=muW_sb[:, a], in_=mu_W[a * P:(a + 1) * P])
+
+        def load_mu(a):
+            nc.sync.dma_start(out=mu_sb[:, a], in_=mu[a * P:(a + 1) * P])
+
+        load_w(0, 0)
+        nc.sync.dma_start(out=h_sb[:, 0:1], in_=hv[:, 0:1])
+        load_w(0, 1)
+        nc.sync.dma_start(out=h_sb[:, 1:2], in_=hv[:, 1:2])
+        nc.sync.dma_start(out=h_sb[:, 2:4], in_=hv[:, 2:4])
+        load_w(1, 0)
+        load_w(1, 1)
+        nc.sync.dma_start(out=muVW_sb[:], in_=mu_VW.rearrange("(a p) o f -> p a (o f)", p=P))
+        load_w(2, 0)
+        load_w(2, 1)
+        nc.sync.dma_start(out=q_sb[:], in_=q.rearrange("(a p) o f -> p a (o f)", p=P))
+        load_w(3, 0)
+        load_w(3, 1)
+        for a in range(4):
+            load_muw(a)
+        load_mu(0)
+        load_mu(1)
+        load_w(4, 0)
+        load_w(4, 1)
+        load_mu(2)
+        load_mu(3)
+        load_w(5, 0)
+        load_w(5, 1)
+
+        srep = const.tile([P, 1024], F32, name="srep")
+        nc.vector.tensor_copy(
+            out=srep[:].rearrange("p (g r t) -> p g r t", g=2, r=P, t=4),
+            in_=s4[:].unsqueeze(2).to_broadcast([P, 2, P, 4]),
+        )
+
+        bias = const.tile([P, 24], F32, name="bias")
+
+        def bias_prep():
+            pb = pm.tile([P, P], BF16, name="pb", tag="mx")
+            nc.tensor.transpose(out=pb[:], in_=bt[:], identity=ident_b[:])
+            nc.vector.tensor_copy(out=bias[:], in_=pb[:, 0:24])
+
+        wbf = {}
+        wt = {}
+        grp = {}
+        wc = {}
+        ws = {}
+        xb = {}
+        xT = {}
+        qo = {}
+        tT = {}
+
+        def ok(c):
+            return 0 <= c < n_cyc
+
+        def turn(dst, words):
+            for g in range(2):
+                for u in range(2):
+                    nc.tensor.transpose(
+                        out=dst[:, u * 256 + g * P:u * 256 + (g + 1) * P],
+                        in_=words[:, 256 * g + u:256 * (g + 1):2],
+                        identity=ident_f[:],
+                    )
+
+        def cast(c, i):
+            if not ok(c):
+                return
+            pr, jj = divmod(i, 2)
+            if (c, pr) not in wbf:
+                wbf[(c, pr)] = wbf_pool.tile([P, 2048], BF16, name="wbf", tag="wbf")
+            nc.scalar.copy(out=wbf[(c, pr)][:, jj * 1024:(jj + 1) * 1024], in_=wb8[(c, pr)][:, jj, :].bitcast(FP8))
+
+        def vcast(c, i):
+            pr, jj = divmod(i, 2)
+            if (c, pr) not in wbf:
+                wbf[(c, pr)] = wbf_pool.tile([P, 2048], BF16, name="wbf", tag="wbf")
+            nc.vector.tensor_copy(out=wbf[(c, pr)][:, jj * 1024:(jj + 1) * 1024], in_=wb8[(c, pr)][:, jj, :].bitcast(FP8))
+
+        def t1(c, i):
+            if not ok(c):
+                return
+            pr, jj = divmod(i, 2)
+            t = pw.tile([P, 512], F32, name="wt", tag="wt")
+            turn(t, wbf[(c, pr)][:, jj * 1024:(jj + 1) * 1024].bitcast(F32))
+            wt[(c, i)] = t
+
+        def scale_out(c, i):
+            if not ok(c):
+                return
+            if i == 0:
+                grp[c] = grp_pool.tile([P, 4096], BF16, name="grp", tag="grp", align_bytes=64)
+            nc.vector.tensor_tensor(
+                out=grp[c][:, i * 1024:(i + 1) * 1024].rearrange("p (x u e) -> p x u e", u=2, e=2),
+                in0=wt[(c, i)][:].bitcast(BF16).rearrange("p (u x e) -> p x u e", u=2, e=2),
+                in1=srep[:].rearrange("p (x u e) -> p x u e", u=2, e=2),
+                op=ALU.mult,
+            )
+
+        def quant(c):
+            if not ok(c):
+                return
+            wc[c] = code_pool.tile([P, 1024], U32, name="wc", tag="wc", align_bytes=64)
+            ws[c] = code_pool.tile([P, 1024], U8, name="ws", tag="ws", align_bytes=64)
+            nc.vector.quantize_mx(out=wc[c][:].bitcast(FP8X4), scales=ws[c][:], in_=grp[c][:])
+
+        def mmb(c, i):
+            if not ok(c):
+                return
+            pr, jj = divmod(i, 2)
+            s, ch = CYC[c][pr]
+            acc = pm.tile([P, 512], F32, name="acc", tag="mx")
+            for g in range(2):
+                c0 = i * 256 + g * P
+                nc.tensor.matmul_mx(
+                    out=acc[:],
+                    lhsT=wc[c][:, c0:c0 + P].bitcast(FP8X4),
+                    lhsT_scale=ws[c][:, c0:c0 + P],
+                    rhs=hc[:, g * 512:(g + 1) * 512].bitcast(FP8X4),
+                    rhs_scale=hs[:, g * 512:(g + 1) * 512],
+                    start=(g == 0),
+                    stop=(g == 1),
+                )
+            t = xb_pool.tile([P, 512], F32, name="xb", tag="xb")
+            rt = s * 8 + 2 * ch + jj
+            nc.scalar.activation(out=t[:], in_=acc[:], func=ACT.Identity, bias=bias[:, rt:rt + 1], scale=1.0)
+            xb[(c, i)] = t
+
+        def t2(c, j):
+            if not ok(c):
+                return
+            pr, hh = divmod(j, 2)
+            s, ch = CYC[c][pr]
+            if s == 2 and ch in IN_PSUM:
+                if hh == 0:
+                    t = px.tile([P, 1024], BF16, name="mv", tag="xT")
+                    for jj in range(2):
+                        for a in range(4):
+                            c0 = 256 * ch + jj * P
+                            nc.tensor.transpose(out=t[:, jj * 512 + a * P:jj * 512 + (a + 1) * P], in_=muVW_sb[:, a, c0:c0 + P], identity=ident_b[:])
+                    xT[(c, j)] = t
+                    xT[(c, j + 1)] = t
+                return
+            t = px.tile([P, 512], F32, name="xT", tag="xT")
+            more = ch in IN_PSUM
+            if s == 0:
+                nc.tensor.matmul(
+                    out=t[:].rearrange("p (a f) -> p a f", a=2),
+                    lhsT=ident_b[:],
+                    rhs=q_sb[:, 2 * hh:2 * hh + 2, 256 * ch:256 * (ch + 1)],
+                    start=True,
+                    stop=False,
+                )
+            for jj in range(2):
+                for a2 in range(2):
+                    a = 2 * hh + a2
+                    dst = t[:, a2 * 256 + jj * P:a2 * 256 + (jj + 1) * P]
+                    src = xb[(c, 2 * pr + jj)][:, a * P:(a + 1) * P]
+                    end = jj == 1 and a2 == 1
+                    if s == 0:
+                        nc.tensor.matmul(out=dst, lhsT=src, rhs=ident_f[:], is_transpose=True, start=False, stop=end and not more)
+                        if more:
+                            nc.tensor.matmul(out=dst, lhsT=tT[(ch, jj)][:, a * P:(a + 1) * P], rhs=ident_f[:], is_transpose=True, start=False, stop=end)
+                    else:
+                        nc.tensor.transpose(out=dst, in_=src, identity=ident_f[:])
+            xT[(c, j)] = t
+
+        q_out_v = out_0.rearrange("(a p) o f -> p a (o f)", p=P)
+        pend = []
+
+        def flush(k):
+            for mo, hh, cs in pend[:k]:
+                for a2 in range(2):
+                    a = 2 * hh + a2
+                    nc.sync.dma_start(out=out_1[a * P:(a + 1) * P, :, cs], in_=mo[:, a2])
+            pend[:k] = []
+
+        def epi(c, j):
+            if not ok(c):
+                return
+            pr, hh = divmod(j, 2)
+            s, i = CYC[c][pr]
+            cs = slice(256 * i, 256 * (i + 1))
+            if s == 2 and i in IN_PSUM:
+                t = tt_pool.tile([P, 512], F32, name="tT", tag="tT")
+                nc.vector.tensor_tensor(out=t[:], in0=xT[(c, j)][:, hh * 512:(hh + 1) * 512], in1=xb[(c, j)][:], op=ALU.mult)
+                tT[(i, hh)] = t
+                return
+            xv = xT[(c, j)][:].rearrange("p (a f) -> p a f", a=2)
+            if s == 0 and i in IN_PSUM:
+                t = qo_pool.tile([P, 2, 256], F32, name="qo", tag="qo")
+                nc.scalar.copy(out=t[:], in_=xv)
+                nc.sync.dma_start(out=q_out_v[:, 2 * hh:2 * hh + 2, cs], in_=t[:])
+                return
+            if s == 1:
+                mo = mo_pool.tile([P, 2, 3, 256], F32, name="mo", tag="mo")
+                nc.vector.tensor_tensor(
+                    out=mo[:],
+                    in0=xv.unsqueeze(2).to_broadcast([P, 2, 3, 256]),
+                    in1=muW_sb[:, 2 * hh:2 * hh + 2, :, cs],
+                    op=ALU.mult,
+                )
+                nc.gpsimd.tensor_tensor(out=mo[:], in0=mo[:], in1=mu_sb[:, 2 * hh:2 * hh + 2, :, cs], op=ALU.add)
+                pend.append((mo, hh, cs))
+            elif s == 2:
+                t = qo_pool.tile([P, 2, 256], F32, name="qo", tag="qo")
+                nc.vector.tensor_tensor(out=t[:], in0=xv, in1=muVW_sb[:, 2 * hh:2 * hh + 2, cs], op=ALU.mult)
+                qo[(i, hh)] = t
+            else:
+                t = qo[(i, hh)]
+                nc.vector.tensor_tensor(out=t[:], in0=xv, in1=t[:], op=ALU.add)
+                nc.sync.dma_start(out=q_out_v[:, 2 * hh:2 * hh + 2, cs], in_=t[:])
+
+        hgrp = const.tile([P, 4096], BF16, name="hgrp", align_bytes=64)
+        hc = const.tile([P, 1024], U32, name="hc", align_bytes=64)
+        hs = const.tile([P, 1024], U8, name="hs", align_bytes=64)
+        hgw = hgrp[:].bitcast(F32).rearrange("p (g a r u) -> p g a r u", g=2, a=4, r=P, u=2)
+
+        def h_turn(a):
+            if a < 3:
+                ht = px.tile([P, 512], F32, name="ht", tag="xT")
+            else:
+                ht = pm.tile([P, 512], F32, name="ht", tag="mx")
+            turn(ht, h_sb[:, a, :].bitcast(F32))
+            nc.scalar.copy(out=hgw[:, :, a], in_=ht[:].rearrange("p (u g r) -> p g r u", u=2, g=2))
+
+        def h_quant():
+            for g in range(2):
+                nc.vector.quantize_mx(
+                    out=hc[:, g * 512:(g + 1) * 512].bitcast(FP8X4),
+                    scales=hs[:, g * 512:(g + 1) * 512],
+                    in_=hgrp[:, g * 2048:(g + 1) * 2048],
+                )
+
+        vcast(0, 0)
+        vcast(0, 1)
+        t1(0, 0)
+        t1(0, 1)
+        vcast(0, 2)
+        vcast(0, 3)
+        h_turn(0)
+        scale_out(0, 0)
+        t1(0, 2)
+        h_turn(1)
+        scale_out(0, 1)
+        t1(0, 3)
+        cast(1, 0)
+        h_turn(2)
+        scale_out(0, 2)
+        cast(1, 1)
+        h_turn(3)
+        scale_out(0, 3)
+        bias_prep()
+        h_quant()
+        for c in range(-1, n_cyc):
+            last2 = c == n_cyc - 2
+            last3 = c == n_cyc - 3
+            flush(1)
+            t1(c + 2, 0)
+            t1(c + 2, 1)
+            cast(c + 2, 2)
+            cast(c + 2, 3)
+            epi(c, 0)
+            t2(c, 3)
+            t1(c + 2, 2)
+            if not last2:
+                quant(c + 1)
+                mmb(c + 1, 0)
+                mmb(c + 1, 1)
+            scale_out(c + 2, 0)
+            t1(c + 2, 3)
+            epi(c, 1)
+            t2(c + 1, 0)
+            if last3:
+                mmb(c + 1, 2)
+                mmb(c + 1, 3)
+                scale_out(c + 2, 1)
+                scale_out(c + 2, 2)
+                scale_out(c + 2, 3)
+            if last3:
+                dummy(2)
+            epi(c, 2)
+            t2(c + 1, 1)
+            if last3:
+                quant(c + 2)
+                mmb(c + 2, 0)
+                mmb(c + 2, 1)
+            cast(c + 3, 0)
+            epi(c, 3)
+            flush(1)
+            if last3:
+                t2(c + 1, 2)
+                mmb(c + 2, 2)
+                mmb(c + 2, 3)
+                flush(1)
+            elif last2:
+                t2(c + 1, 2)
+            else:
+                mmb(c + 1, 2)
+                mmb(c + 1, 3)
+                cast(c + 3, 1)
+                scale_out(c + 2, 1)
+                t2(c + 1, 2)
+                scale_out(c + 2, 2)
+                scale_out(c + 2, 3)
+                if ok(c + 2):
+                    flush(1)
+        flush(len(pend))

@@ -47,6 +47,8 @@ def tile_painnmixing_pb_kernel(tc, h, mu_W, mu_VW, q, mu, W2_bytes, W2_scale, b2
         if MANUAL:
             ctx.enter_context(tc.manual_schedule())
 
+        zer = const.tile([P, 512], BF16, name="zer")
+        nc.vector.memset(zer[:], 0.0)
         s4 = const.tile([P, 2, 4], F32, name="s4")
         nc.sync.dma_start(out=s4[:], in_=W2_scale.rearrange("o (g p t) -> p (o g) t", g=2, p=P, t=4))
         bt = const.tile([P, P], BF16, name="bt")
@@ -63,15 +65,13 @@ def tile_painnmixing_pb_kernel(tc, h, mu_W, mu_VW, q, mu, W2_bytes, W2_scale, b2
         ident_b = const.tile([P, P], BF16, name="ident_b")
         make_identity(nc, ident_b[:])
 
-        zer = const.tile([P, 512], BF16, name="zer")
-        nc.vector.memset(zer[:], 0.0)
 
         def dummy(k):
             for r in range(k):
                 dm = pm.tile([P, 512], F32, name="dm", tag="mx")
-                nc.tensor.matmul(out=dm[:], lhsT=ident_b[:], rhs=zer[:], start=True, stop=True)
+                nc.tensor.matmul(out=dm[:], lhsT=zer[:, 0:P], rhs=zer[:], start=True, stop=True)
 
-        dummy(4)
+        dummy(6)
         w2v = W2_bytes.rearrange("(n p) k -> p n k", p=P)
         wb8 = {}
 
@@ -120,7 +120,7 @@ def tile_painnmixing_pb_kernel(tc, h, mu_W, mu_VW, q, mu, W2_bytes, W2_scale, b2
         load_w(5, 1)
 
         srep = const.tile([P, 1024], F32, name="srep")
-        nc.vector.tensor_copy(
+        nc.scalar.copy(
             out=srep[:].rearrange("p (g r t) -> p g r t", g=2, r=P, t=4),
             in_=s4[:].unsqueeze(2).to_broadcast([P, 2, P, 4]),
         )
@@ -327,20 +327,20 @@ def tile_painnmixing_pb_kernel(tc, h, mu_W, mu_VW, q, mu, W2_bytes, W2_scale, b2
         vcast(0, 1)
         t1(0, 0)
         t1(0, 1)
-        vcast(0, 2)
-        vcast(0, 3)
-        h_turn(0)
+        cast(0, 2)
+        cast(0, 3)
         scale_out(0, 0)
+        h_turn(0)
         t1(0, 2)
-        h_turn(1)
         scale_out(0, 1)
+        h_turn(1)
         t1(0, 3)
-        cast(1, 0)
-        h_turn(2)
         scale_out(0, 2)
-        cast(1, 1)
+        h_turn(2)
         h_turn(3)
         scale_out(0, 3)
+        cast(1, 0)
+        cast(1, 1)
         bias_prep()
         h_quant()
         for c in range(-1, n_cyc):

@@ -47,18 +47,16 @@ def tile_painnmixing_pb_kernel(tc, h, mu_W, mu_VW, q, mu, W2_bytes, W2_scale, b2
         if MANUAL:
             ctx.enter_context(tc.manual_schedule())
 
-        zer = const.tile([P, 512], BF16, name="zer")
-        nc.vector.memset(zer[:], 0.0)
-        s4 = const.tile([P, 2, 4], F32, name="s4")
-        nc.sync.dma_start(out=s4[:], in_=W2_scale.rearrange("o (g p t) -> p (o g) t", g=2, p=P, t=4))
-        bt = const.tile([P, P], BF16, name="bt")
-        nc.vector.memset(bt[:], 0.0)
-        nc.scalar.dma_start(out=bt[0:24, :], in_=b2.rearrange("(j p) -> j p", p=P))
-
         warm = const.tile([P, 1], F32, name="warm")
         warm2 = const.tile([P, 1], F32, name="warm2")
         nc.vector.memset(warm[:], 0.0)
         nc.scalar.activation(out=warm2[:], in_=warm[:], func=ACT.Identity)
+        zer = const.tile([P, 512], BF16, name="zer")
+        nc.vector.memset(zer[:], 0.0)
+        s4 = const.tile([P, 2, 4], F32, name="s4")
+        bt = const.tile([P, P], BF16, name="bt")
+        nc.vector.memset(bt[:], 0.0)
+        nc.scalar.dma_start(out=bt[0:24, :], in_=b2.rearrange("(j p) -> j p", p=P))
 
         ident_f = const.tile([P, P], F32, name="ident_f")
         make_identity(nc, ident_f[:])
@@ -95,9 +93,13 @@ def tile_painnmixing_pb_kernel(tc, h, mu_W, mu_VW, q, mu, W2_bytes, W2_scale, b2
         def load_mu(a):
             nc.sync.dma_start(out=mu_sb[:, a], in_=mu[a * P:(a + 1) * P])
 
-        load_w(0, 0)
-        nc.sync.dma_start(out=h_sb[:, 0:1], in_=hv[:, 0:1])
+        wb8[(0, 0)] = inp.tile([P, 2, 1024], U8, name="wb8_0_0")
+        for jj in range(2):
+            nc.sync.dma_start(out=wb8[(0, 0)][:, jj:jj + 1, :], in_=w2v[:, CYC[0][0][0] * 8 + 2 * CYC[0][0][1] + jj:CYC[0][0][0] * 8 + 2 * CYC[0][0][1] + jj + 1, :])
+            if jj == 0:
+                nc.sync.dma_start(out=s4[:], in_=W2_scale.rearrange("o (g p t) -> p (o g) t", g=2, p=P, t=4))
         load_w(0, 1)
+        nc.sync.dma_start(out=h_sb[:, 0:1], in_=hv[:, 0:1])
         nc.sync.dma_start(out=h_sb[:, 1:2], in_=hv[:, 1:2])
         nc.sync.dma_start(out=h_sb[:, 2:4], in_=hv[:, 2:4])
         load_w(1, 0)
@@ -327,7 +329,7 @@ def tile_painnmixing_pb_kernel(tc, h, mu_W, mu_VW, q, mu, W2_bytes, W2_scale, b2
         vcast(0, 1)
         t1(0, 0)
         t1(0, 1)
-        cast(0, 2)
+        vcast(0, 2)
         cast(0, 3)
         scale_out(0, 0)
         h_turn(0)
@@ -341,8 +343,9 @@ def tile_painnmixing_pb_kernel(tc, h, mu_W, mu_VW, q, mu, W2_bytes, W2_scale, b2
         scale_out(0, 3)
         cast(1, 0)
         cast(1, 1)
-        bias_prep()
+        dummy(3)
         h_quant()
+        bias_prep()
         for c in range(-1, n_cyc):
             last2 = c == n_cyc - 2
             last3 = c == n_cyc - 3

@@ -293,7 +293,8 @@ def tile_painnmixing_pb_kernel(tc, h, mu_W, mu_VW, q, mu, W2_bytes, W2_scale, b2
                     in1=muW_sb[:, 2 * hh:2 * hh + 2, :, cs],
                     op=ALU.mult,
                 )
-                nc.gpsimd.tensor_tensor(out=mo[:], in0=mo[:], in1=mu_sb[:, 2 * hh:2 * hh + 2, :, cs], op=ALU.add)
+                for a2 in range(2):
+                    nc.gpsimd.tensor_tensor(out=mo[:, a2], in0=mo[:, a2], in1=mu_sb[:, 2 * hh + a2, :, cs], op=ALU.add)
                 pend.append((mo, hh, cs))
             elif s == 2:
                 t = qo_pool.tile([P, 2, 256], F32, name="qo", tag="qo")

@@ -25,6 +25,9 @@ CYC = [
 ]
 IN_PSUM = (0, 1)
 MANUAL = True
+N_G = [0, 1, 1, 1, 1, 0]
+G_AT = {(-1, 2): [(3, 0)], (-1, 3): [(4, 0)]}
+G_TILES = [(c, i) for c in range(6) for i in range(N_G[c])]
 
 
 def tile_painnmixing_pb_kernel(tc, h, mu_W, mu_VW, q, mu, W2_bytes, W2_scale, b2, out_0, out_1):
@@ -34,8 +37,9 @@ def tile_painnmixing_pb_kernel(tc, h, mu_W, mu_VW, q, mu, W2_bytes, W2_scale, b2
     with ExitStack() as ctx:
         const = ctx.enter_context(tc.tile_pool(name="const", bufs=1))
         inp = ctx.enter_context(tc.tile_pool(name="inp", bufs=1))
-        wbf_pool = ctx.enter_context(tc.tile_pool(name="wbfp", bufs=5))
+        wbf_pool = ctx.enter_context(tc.tile_pool(name="wbfp", bufs=4))
         grp_pool = ctx.enter_context(tc.tile_pool(name="grpp", bufs=3))
+        gbf_pool = ctx.enter_context(tc.tile_pool(name="gbfp", bufs=1))
         code_pool = ctx.enter_context(tc.tile_pool(name="codep", bufs=2))
         xb_pool = ctx.enter_context(tc.tile_pool(name="xbp", bufs=6))
         mo_pool = ctx.enter_context(tc.tile_pool(name="mop", bufs=4))
@@ -69,7 +73,7 @@ def tile_painnmixing_pb_kernel(tc, h, mu_W, mu_VW, q, mu, W2_bytes, W2_scale, b2
                 dm = pm.tile([P, 512], F32, name="dm", tag="mx")
                 nc.tensor.matmul(out=dm[:], lhsT=zer[:, 0:P], rhs=zer[:], start=True, stop=True)
 
-        dummy(6)
+        dummy(3)
         w2v = W2_bytes.rearrange("(n p) k -> p n k", p=P)
         wb8 = {}
 
@@ -87,6 +91,8 @@ def tile_painnmixing_pb_kernel(tc, h, mu_W, mu_VW, q, mu, W2_bytes, W2_scale, b2
         muVW_sb = inp.tile([P, 4, 1024], BF16, name="muVW_sb")
         q_sb = inp.tile([P, 4, 1024], BF16, name="q_sb")
 
+        srow = const.tile([P, 1024], F32, name="srow")
+
         def load_muw(a):
             nc.sync.dma_start(out=muW_sb[:, a], in_=mu_W[a * P:(a + 1) * P])
 
@@ -99,33 +105,28 @@ def tile_painnmixing_pb_kernel(tc, h, mu_W, mu_VW, q, mu, W2_bytes, W2_scale, b2
             if jj == 0:
                 nc.sync.dma_start(out=s4[:], in_=W2_scale.rearrange("o (g p t) -> p (o g) t", g=2, p=P, t=4))
         load_w(0, 1)
+        load_w(1, 0)
+        nc.sync.dma_start(out=srow[:], in_=W2_scale.rearrange("o k -> (o k)").partition_broadcast(P))
         nc.sync.dma_start(out=h_sb[:, 0:1], in_=hv[:, 0:1])
         nc.sync.dma_start(out=h_sb[:, 1:2], in_=hv[:, 1:2])
         nc.sync.dma_start(out=h_sb[:, 2:4], in_=hv[:, 2:4])
-        load_w(1, 0)
-        load_w(1, 1)
-        nc.sync.dma_start(out=muVW_sb[:], in_=mu_VW.rearrange("(a p) o f -> p a (o f)", p=P))
         load_w(2, 0)
-        load_w(2, 1)
-        nc.sync.dma_start(out=q_sb[:], in_=q.rearrange("(a p) o f -> p a (o f)", p=P))
+        load_w(1, 1)
         load_w(3, 0)
+        nc.sync.dma_start(out=muVW_sb[:], in_=mu_VW.rearrange("(a p) o f -> p a (o f)", p=P))
+        load_w(2, 1)
+        load_w(4, 0)
+        nc.sync.dma_start(out=q_sb[:], in_=q.rearrange("(a p) o f -> p a (o f)", p=P))
         load_w(3, 1)
         for a in range(4):
             load_muw(a)
         load_mu(0)
         load_mu(1)
-        load_w(4, 0)
         load_w(4, 1)
         load_mu(2)
         load_mu(3)
         load_w(5, 0)
         load_w(5, 1)
-
-        srep = const.tile([P, 1024], F32, name="srep")
-        nc.scalar.copy(
-            out=srep[:].rearrange("p (g r t) -> p g r t", g=2, r=P, t=4),
-            in_=s4[:].unsqueeze(2).to_broadcast([P, 2, P, 4]),
-        )
 
         bias = const.tile([P, 24], F32, name="bias")
 
@@ -135,6 +136,7 @@ def tile_painnmixing_pb_kernel(tc, h, mu_W, mu_VW, q, mu, W2_bytes, W2_scale, b2
             nc.vector.tensor_copy(out=bias[:], in_=pb[:, 0:24])
 
         wbf = {}
+        gbf = {}
         wt = {}
         grp = {}
         wc = {}
@@ -159,6 +161,8 @@ def tile_painnmixing_pb_kernel(tc, h, mu_W, mu_VW, q, mu, W2_bytes, W2_scale, b2
         def cast(c, i):
             if not ok(c):
                 return
+            if (c, i) in G_TILES:
+                return
             pr, jj = divmod(i, 2)
             if (c, pr) not in wbf:
                 wbf[(c, pr)] = wbf_pool.tile([P, 2048], BF16, name="wbf", tag="wbf")
@@ -170,12 +174,23 @@ def tile_painnmixing_pb_kernel(tc, h, mu_W, mu_VW, q, mu, W2_bytes, W2_scale, b2
                 wbf[(c, pr)] = wbf_pool.tile([P, 2048], BF16, name="wbf", tag="wbf")
             nc.vector.tensor_copy(out=wbf[(c, pr)][:, jj * 1024:(jj + 1) * 1024], in_=wb8[(c, pr)][:, jj, :].bitcast(FP8))
 
+        def g_scale(c, i):
+            pr, jj = divmod(i, 2)
+            gbf[(c, i)] = gbf_pool.tile([P, 1024], BF16, name="gbf_%d_%d" % (c, i))
+            nc.scalar.copy(out=gbf[(c, i)][:], in_=wb8[(c, pr)][:, jj, :].bitcast(FP8))
+            for hf in range(2):
+                cs = slice(512 * hf, 512 * (hf + 1))
+                nc.gpsimd.tensor_tensor(out=gbf[(c, i)][:, cs], in0=gbf[(c, i)][:, cs], in1=srow[:, cs], op=ALU.mult)
+
         def t1(c, i):
             if not ok(c):
                 return
             pr, jj = divmod(i, 2)
             t = pw.tile([P, 512], F32, name="wt", tag="wt")
-            turn(t, wbf[(c, pr)][:, jj * 1024:(jj + 1) * 1024].bitcast(F32))
+            if (c, i) in G_TILES:
+                turn(t, gbf[(c, i)][:].bitcast(F32))
+            else:
+                turn(t, wbf[(c, pr)][:, jj * 1024:(jj + 1) * 1024].bitcast(F32))
             wt[(c, i)] = t
 
         def scale_out(c, i):
@@ -183,10 +198,16 @@ def tile_painnmixing_pb_kernel(tc, h, mu_W, mu_VW, q, mu, W2_bytes, W2_scale, b2
                 return
             if i == 0:
                 grp[c] = grp_pool.tile([P, 4096], BF16, name="grp", tag="grp", align_bytes=64)
+            if (c, i) in G_TILES:
+                nc.scalar.copy(
+                    out=grp[c][:, i * 1024:(i + 1) * 1024].bitcast(F32).rearrange("p (x u) -> p x u", u=2),
+                    in_=wt[(c, i)][:].rearrange("p (u x) -> p x u", u=2),
+                )
+                return
             nc.vector.tensor_tensor(
-                out=grp[c][:, i * 1024:(i + 1) * 1024].rearrange("p (x u e) -> p x u e", u=2, e=2),
-                in0=wt[(c, i)][:].bitcast(BF16).rearrange("p (u x e) -> p x u e", u=2, e=2),
-                in1=srep[:].rearrange("p (x u e) -> p x u e", u=2, e=2),
+                out=grp[c][:, i * 1024:(i + 1) * 1024].rearrange("p (g r u e) -> p g r u e", g=2, u=2, e=2),
+                in0=wt[(c, i)][:].bitcast(BF16).rearrange("p (u g r e) -> p g r u e", u=2, g=2, e=2),
+                in1=s4[:].rearrange("p g (u e) -> p g u e", u=2).unsqueeze(2).to_broadcast([P, 2, P, 2, 2]),
                 op=ALU.mult,
             )
 
@@ -219,7 +240,7 @@ def tile_painnmixing_pb_kernel(tc, h, mu_W, mu_VW, q, mu, W2_bytes, W2_scale, b2
             nc.scalar.activation(out=t[:], in_=acc[:], func=ACT.Identity, bias=bias[:, rt:rt + 1], scale=1.0)
             xb[(c, i)] = t
 
-        def t2(c, j):
+        def t2(c, j, in_pw=False):
             if not ok(c):
                 return
             pr, hh = divmod(j, 2)
@@ -234,7 +255,10 @@ def tile_painnmixing_pb_kernel(tc, h, mu_W, mu_VW, q, mu, W2_bytes, W2_scale, b2
                     xT[(c, j)] = t
                     xT[(c, j + 1)] = t
                 return
-            t = px.tile([P, 512], F32, name="xT", tag="xT")
+            if in_pw:
+                t = pw.tile([P, 512], F32, name="xT", tag="wt")
+            else:
+                t = px.tile([P, 512], F32, name="xT", tag="xT")
             more = ch in IN_PSUM
             if s == 0:
                 nc.tensor.matmul(
@@ -261,12 +285,14 @@ def tile_painnmixing_pb_kernel(tc, h, mu_W, mu_VW, q, mu, W2_bytes, W2_scale, b2
         q_out_v = out_0.rearrange("(a p) o f -> p a (o f)", p=P)
         pend = []
 
+        def flush_half():
+            mo, a, cs = pend[0]
+            nc.sync.dma_start(out=out_1[a * P:(a + 1) * P, :, cs], in_=mo[:, a % 2])
+            pend[:1] = []
+
         def flush(k):
-            for mo, hh, cs in pend[:k]:
-                for a2 in range(2):
-                    a = 2 * hh + a2
-                    nc.sync.dma_start(out=out_1[a * P:(a + 1) * P, :, cs], in_=mo[:, a2])
-            pend[:k] = []
+            for r in range(min(2 * k, len(pend))):
+                flush_half()
 
         def epi(c, j):
             if not ok(c):
@@ -281,12 +307,12 @@ def tile_painnmixing_pb_kernel(tc, h, mu_W, mu_VW, q, mu, W2_bytes, W2_scale, b2
                 return
             xv = xT[(c, j)][:].rearrange("p (a f) -> p a f", a=2)
             if s == 0 and i in IN_PSUM:
-                t = qo_pool.tile([P, 2, 256], F32, name="qo", tag="qo")
+                t = qo_pool.tile([P, 2, 256], F32, name="qo", tag="qo", align_bytes=256)
                 nc.scalar.copy(out=t[:], in_=xv)
                 nc.sync.dma_start(out=q_out_v[:, 2 * hh:2 * hh + 2, cs], in_=t[:])
                 return
             if s == 1:
-                mo = mo_pool.tile([P, 2, 3, 256], F32, name="mo", tag="mo")
+                mo = mo_pool.tile([P, 2, 3, 256], F32, name="mo", tag="mo", align_bytes=256)
                 nc.vector.tensor_tensor(
                     out=mo[:],
                     in0=xv.unsqueeze(2).to_broadcast([P, 2, 3, 256]),
@@ -295,9 +321,9 @@ def tile_painnmixing_pb_kernel(tc, h, mu_W, mu_VW, q, mu, W2_bytes, W2_scale, b2
                 )
                 for a2 in range(2):
                     nc.gpsimd.tensor_tensor(out=mo[:, a2], in0=mo[:, a2], in1=mu_sb[:, 2 * hh + a2, :, cs], op=ALU.add)
-                pend.append((mo, hh, cs))
+                pend.extend([(mo, 2 * hh, cs), (mo, 2 * hh + 1, cs)])
             elif s == 2:
-                t = qo_pool.tile([P, 2, 256], F32, name="qo", tag="qo")
+                t = qo_pool.tile([P, 2, 256], F32, name="qo", tag="qo", align_bytes=256)
                 nc.vector.tensor_tensor(out=t[:], in0=xv, in1=muVW_sb[:, 2 * hh:2 * hh + 2, cs], op=ALU.mult)
                 qo[(i, hh)] = t
             else:
@@ -331,73 +357,124 @@ def tile_painnmixing_pb_kernel(tc, h, mu_W, mu_VW, q, mu, W2_bytes, W2_scale, b2
         t1(0, 0)
         t1(0, 1)
         vcast(0, 2)
+        t1(0, 2)
         cast(0, 3)
+        g_scale(1, 0)
+        cast(1, 1)
         scale_out(0, 0)
         h_turn(0)
-        t1(0, 2)
         scale_out(0, 1)
-        h_turn(1)
         t1(0, 3)
+        h_turn(1)
         scale_out(0, 2)
         h_turn(2)
         h_turn(3)
         scale_out(0, 3)
-        cast(1, 0)
-        cast(1, 1)
-        dummy(3)
+        cast(1, 2)
+        cast(1, 3)
+        g_scale(2, 0)
+        dummy(2)
+        quant(0)
         h_quant()
         bias_prep()
-        for c in range(-1, n_cyc):
-            last2 = c == n_cyc - 2
-            last3 = c == n_cyc - 3
+        def a_tile(c, n):
+            return N_G[c] + n if ok(c) and N_G[c] + n < 4 else None
+
+        def casts(c, ns):
+            for n in ns:
+                i = a_tile(c, n)
+                if i is not None:
+                    cast(c, i)
+
+        def g_at(c, n):
+            for ci in G_AT.get((c, n), []):
+                g_scale(*ci)
+
+        for c in range(-1, 3):
+            ng = N_G[c + 2]
             flush(1)
             t1(c + 2, 0)
+            if ng > 0:
+                scale_out(c + 2, 0)
             t1(c + 2, 1)
-            cast(c + 2, 2)
-            cast(c + 2, 3)
+            if ng > 1:
+                scale_out(c + 2, 1)
+            if c >= 0:
+                casts(c + 2, [2, 3])
+            g_at(c, 0)
             epi(c, 0)
             t2(c, 3)
             t1(c + 2, 2)
-            if not last2:
+            if c >= 0:
                 quant(c + 1)
-                mmb(c + 1, 0)
-                mmb(c + 1, 1)
-            scale_out(c + 2, 0)
+            mmb(c + 1, 0)
+            mmb(c + 1, 1)
+            if ng == 0:
+                scale_out(c + 2, 0)
             t1(c + 2, 3)
+            g_at(c, 1)
             epi(c, 1)
             t2(c + 1, 0)
-            if last3:
-                mmb(c + 1, 2)
-                mmb(c + 1, 3)
-                scale_out(c + 2, 1)
-                scale_out(c + 2, 2)
-                scale_out(c + 2, 3)
-            if last3:
-                dummy(2)
             epi(c, 2)
             t2(c + 1, 1)
-            if last3:
-                quant(c + 2)
-                mmb(c + 2, 0)
-                mmb(c + 2, 1)
-            cast(c + 3, 0)
+            casts(c + 3, [0])
+            g_at(c, 2)
             epi(c, 3)
             flush(1)
-            if last3:
-                t2(c + 1, 2)
-                mmb(c + 2, 2)
-                mmb(c + 2, 3)
-                flush(1)
-            elif last2:
-                t2(c + 1, 2)
-            else:
-                mmb(c + 1, 2)
-                mmb(c + 1, 3)
-                cast(c + 3, 1)
+            mmb(c + 1, 2)
+            mmb(c + 1, 3)
+            casts(c + 3, [1])
+            g_at(c, 3)
+            if ng < 2:
                 scale_out(c + 2, 1)
-                t2(c + 1, 2)
-                scale_out(c + 2, 2)
-                scale_out(c + 2, 3)
-                if ok(c + 2):
-                    flush(1)
-        flush(len(pend))
+            t2(c + 1, 2)
+            scale_out(c + 2, 2)
+            scale_out(c + 2, 3)
+            flush(1)
+
+        flush(1)
+        t1(5, 0)
+        t1(5, 1)
+        casts(5, [2, 3])
+        epi(3, 0)
+        t2(3, 3)
+        t1(5, 2)
+        quant(4)
+        mmb(4, 0)
+        mmb(4, 1)
+        scale_out(5, 0)
+        t1(5, 3)
+        epi(3, 1)
+        flush(1)
+        t2(4, 0)
+        mmb(4, 2)
+        mmb(4, 3)
+        scale_out(5, 1)
+        scale_out(5, 2)
+        scale_out(5, 3)
+        epi(3, 2)
+        flush(1)
+        t2(4, 1)
+        t2(4, 2, True)
+        quant(5)
+        t2(4, 3, True)
+        mmb(5, 0)
+        mmb(5, 1)
+        epi(3, 3)
+        flush(1)
+        epi(4, 0)
+        mmb(5, 2)
+        mmb(5, 3)
+        epi(4, 1)
+        t2(5, 0)
+        epi(4, 2)
+        t2(5, 1)
+        epi(4, 3)
+        t2(5, 2)
+        t2(5, 3, True)
+        epi(5, 0)
+        epi(5, 1)
+        flush_half()
+        epi(5, 2)
+        epi(5, 3)
+        flush_half()

@@ -25,8 +25,8 @@ CYC = [
 ]
 IN_PSUM = (0, 1)
 MANUAL = True
-N_G = [0, 1, 1, 1, 1, 0]
-G_AT = {(-1, 2): [(3, 0)], (-1, 3): [(4, 0)]}
+N_G = [0, 0, 0, 0, 0, 0]
+G_AT = {}
 G_TILES = [(c, i) for c in range(6) for i in range(N_G[c])]
 
 
@@ -106,7 +106,6 @@ def tile_painnmixing_pb_kernel(tc, h, mu_W, mu_VW, q, mu, W2_bytes, W2_scale, b2
                 nc.sync.dma_start(out=s4[:], in_=W2_scale.rearrange("o (g p t) -> p (o g) t", g=2, p=P, t=4))
         load_w(0, 1)
         load_w(1, 0)
-        nc.sync.dma_start(out=srow[:], in_=W2_scale.rearrange("o k -> (o k)").partition_broadcast(P))
         nc.sync.dma_start(out=h_sb[:, 0:1], in_=hv[:, 0:1])
         nc.sync.dma_start(out=h_sb[:, 1:2], in_=hv[:, 1:2])
         nc.sync.dma_start(out=h_sb[:, 2:4], in_=hv[:, 2:4])
@@ -359,7 +358,7 @@ def tile_painnmixing_pb_kernel(tc, h, mu_W, mu_VW, q, mu, W2_bytes, W2_scale, b2
         vcast(0, 2)
         t1(0, 2)
         cast(0, 3)
-        g_scale(1, 0)
+        cast(1, 0)
         cast(1, 1)
         scale_out(0, 0)
         h_turn(0)
@@ -372,7 +371,6 @@ def tile_painnmixing_pb_kernel(tc, h, mu_W, mu_VW, q, mu, W2_bytes, W2_scale, b2
         scale_out(0, 3)
         cast(1, 2)
         cast(1, 3)
-        g_scale(2, 0)
         dummy(2)
         quant(0)
         h_quant()

@@ -73,7 +73,7 @@ def tile_painnmixing_pb_kernel(tc, h, mu_W, mu_VW, q, mu, W2_bytes, W2_scale, b2
                 dm = pm.tile([P, 512], F32, name="dm", tag="mx")
                 nc.tensor.matmul(out=dm[:], lhsT=zer[:, 0:P], rhs=zer[:], start=True, stop=True)
 
-        dummy(3)
+        dummy(5)
         w2v = W2_bytes.rearrange("(n p) k -> p n k", p=P)
         wb8 = {}
 
@@ -355,16 +355,20 @@ def tile_painnmixing_pb_kernel(tc, h, mu_W, mu_VW, q, mu, W2_bytes, W2_scale, b2
         vcast(0, 1)
         t1(0, 0)
         t1(0, 1)
+        dummy(1)
         vcast(0, 2)
         t1(0, 2)
+        dummy(1)
         cast(0, 3)
         cast(1, 0)
         cast(1, 1)
         scale_out(0, 0)
         h_turn(0)
+        dummy(1)
         scale_out(0, 1)
         t1(0, 3)
         h_turn(1)
+        dummy(1)
         scale_out(0, 2)
         h_turn(2)
         h_turn(3)

@@ -195,7 +195,7 @@ def tile_painnmixing_pb_kernel(tc, h, mu_W, mu_VW, q, mu, W2_bytes, W2_scale, b2
         def scale_out(c, i):
             if not ok(c):
                 return
-            if i == 0:
+            if c not in grp:
                 grp[c] = grp_pool.tile([P, 4096], BF16, name="grp", tag="grp", align_bytes=64)
             if (c, i) in G_TILES:
                 nc.scalar.copy(
@@ -209,6 +209,15 @@ def tile_painnmixing_pb_kernel(tc, h, mu_W, mu_VW, q, mu, W2_bytes, W2_scale, b2
                 in1=s4[:].rearrange("p g (u e) -> p g u e", u=2).unsqueeze(2).to_broadcast([P, 2, P, 2, 2]),
                 op=ALU.mult,
             )
+
+        def s_scale(c, i, gs):
+            if c not in grp:
+                grp[c] = grp_pool.tile([P, 4096], BF16, name="grp", tag="grp", align_bytes=64)
+            turned = wt[(c, i)][:].bitcast(BF16).rearrange("p (u g r e) -> p u g r e", u=2, g=2, e=2)
+            dst = grp[c][:, i * 1024:(i + 1) * 1024].rearrange("p (g r t) -> p g r t", g=2, t=4)
+            for g in gs:
+                for t in range(4):
+                    nc.scalar.activation(out=dst[:, g, :, t], in_=turned[:, t // 2, g, :, t % 2], func=ACT.Copy, scale=s4[:, g, t:t + 1])
 
         def quant(c):
             if not ok(c):
@@ -438,12 +447,14 @@ def tile_painnmixing_pb_kernel(tc, h, mu_W, mu_VW, q, mu, W2_bytes, W2_scale, b2
         t1(5, 0)
         t1(5, 1)
         casts(5, [2, 3])
+        s_scale(5, 1, [0])
         epi(3, 0)
         t2(3, 3)
         t1(5, 2)
         quant(4)
         mmb(4, 0)
         mmb(4, 1)
+        s_scale(5, 1, [1])
         scale_out(5, 0)
         t1(5, 3)
         epi(3, 1)
@@ -451,7 +462,6 @@ def tile_painnmixing_pb_kernel(tc, h, mu_W, mu_VW, q, mu, W2_bytes, W2_scale, b2
         t2(4, 0)
         mmb(4, 2)
         mmb(4, 3)
-        scale_out(5, 1)
         scale_out(5, 2)
         scale_out(5, 3)
         epi(3, 2)

@@ -37,7 +37,7 @@ def tile_painnmixing_pb_kernel(tc, h, mu_W, mu_VW, q, mu, W2_bytes, W2_scale, b2
     with ExitStack() as ctx:
         const = ctx.enter_context(tc.tile_pool(name="const", bufs=1))
         inp = ctx.enter_context(tc.tile_pool(name="inp", bufs=1))
-        wbf_pool = ctx.enter_context(tc.tile_pool(name="wbfp", bufs=4))
+        wbf_pool = ctx.enter_context(tc.tile_pool(name="wbfp", bufs=6))
         grp_pool = ctx.enter_context(tc.tile_pool(name="grpp", bufs=3))
         gbf_pool = ctx.enter_context(tc.tile_pool(name="gbfp", bufs=1))
         code_pool = ctx.enter_context(tc.tile_pool(name="codep", bufs=2))
@@ -218,6 +218,18 @@ def tile_painnmixing_pb_kernel(tc, h, mu_W, mu_VW, q, mu, W2_bytes, W2_scale, b2
             for g in gs:
                 for t in range(4):
                     nc.scalar.activation(out=dst[:, g, :, t], in_=turned[:, t // 2, g, :, t % 2], func=ACT.Copy, scale=s4[:, g, t:t + 1])
+
+        def g_scale(c, i):
+            if c not in grp:
+                grp[c] = grp_pool.tile([P, 4096], BF16, name="grp", tag="grp", align_bytes=64)
+            part = grp[c][:, i * 1024:(i + 1) * 1024]
+            nc.scalar.copy(
+                out=part.bitcast(F32).rearrange("p (x u) -> p x u", u=2),
+                in_=wt[(c, i)][:].rearrange("p (u x) -> p x u", u=2),
+            )
+            for g in range(2):
+                half = part[:, 512 * g:512 * (g + 1)].rearrange("p (r t) -> p r t", t=4)
+                nc.gpsimd.tensor_tensor(out=half, in0=half, in1=s4[:, g:g + 1, :].to_broadcast([P, P, 4]), op=ALU.mult)
 
         def quant(c):
             if not ok(c):
@@ -404,14 +416,15 @@ def tile_painnmixing_pb_kernel(tc, h, mu_W, mu_VW, q, mu, W2_bytes, W2_scale, b2
         for c in range(-1, 3):
             ng = N_G[c + 2]
             flush(1)
-            t1(c + 2, 0)
-            if ng > 0:
-                scale_out(c + 2, 0)
+            if c == -1:
+                t1(1, 0)
             t1(c + 2, 1)
             if ng > 1:
                 scale_out(c + 2, 1)
+            if c == 0:
+                g_scale(2, 0)
             if c >= 0:
-                casts(c + 2, [2, 3])
+                casts(c + 2, [2, 3] if c > 0 else [3])
             g_at(c, 0)
             epi(c, 0)
             t2(c, 3)
@@ -420,7 +433,7 @@ def tile_painnmixing_pb_kernel(tc, h, mu_W, mu_VW, q, mu, W2_bytes, W2_scale, b2
                 quant(c + 1)
             mmb(c + 1, 0)
             mmb(c + 1, 1)
-            if ng == 0:
+            if c != 0:
                 scale_out(c + 2, 0)
             t1(c + 2, 3)
             g_at(c, 1)
@@ -434,17 +447,17 @@ def tile_painnmixing_pb_kernel(tc, h, mu_W, mu_VW, q, mu, W2_bytes, W2_scale, b2
             flush(1)
             mmb(c + 1, 2)
             mmb(c + 1, 3)
-            casts(c + 3, [1])
+            casts(c + 3, [1] if c >= 0 else [1, 2])
             g_at(c, 3)
             if ng < 2:
                 scale_out(c + 2, 1)
+            t1(c + 3, 0)
             t2(c + 1, 2)
             scale_out(c + 2, 2)
             scale_out(c + 2, 3)
             flush(1)
 
         flush(1)
-        t1(5, 0)
         t1(5, 1)
         casts(5, [2, 3])
         s_scale(5, 1, [0])

@@ -79,17 +79,17 @@ def tile_painnmixing_pb_kernel(tc, h, mu_W, mu_VW, q, mu, W2_bytes, W2_scale, b2
 
         def load_w(c, pr):
             s, i = CYC[c][pr]
-            t = inp.tile([P, 2, 1024], U8, name="wb8_%d_%d" % (c, pr))
+            t = inp.tile([P, 2, 1024], U8, name="wb8_%d_%d" % (c, pr), align_bytes=256)
             rt = s * 8 + 2 * i
             nc.sync.dma_start(out=t[:], in_=w2v[:, rt:rt + 2, :])
             wb8[(c, pr)] = t
 
-        h_sb = inp.tile([P, 4, 1024], BF16, name="h_sb")
+        h_sb = inp.tile([P, 4, 1024], BF16, name="h_sb", align_bytes=256)
         hv = h.rearrange("(a p) o k -> p a (o k)", p=P)
-        muW_sb = inp.tile([P, 4, 3, 1024], BF16, name="muW_sb")
-        mu_sb = inp.tile([P, 4, 3, 1024], BF16, name="mu_sb")
-        muVW_sb = inp.tile([P, 4, 1024], BF16, name="muVW_sb")
-        q_sb = inp.tile([P, 4, 1024], BF16, name="q_sb")
+        muW_sb = inp.tile([P, 4, 3, 1024], BF16, name="muW_sb", align_bytes=256)
+        mu_sb = inp.tile([P, 4, 3, 1024], BF16, name="mu_sb", align_bytes=256)
+        muVW_sb = inp.tile([P, 4, 1024], BF16, name="muVW_sb", align_bytes=256)
+        q_sb = inp.tile([P, 4, 1024], BF16, name="q_sb", align_bytes=256)
 
         srow = const.tile([P, 1024], F32, name="srow")
 
@@ -99,7 +99,7 @@ def tile_painnmixing_pb_kernel(tc, h, mu_W, mu_VW, q, mu, W2_bytes, W2_scale, b2
         def load_mu(a):
             nc.sync.dma_start(out=mu_sb[:, a], in_=mu[a * P:(a + 1) * P])
 
-        wb8[(0, 0)] = inp.tile([P, 2, 1024], U8, name="wb8_0_0")
+        wb8[(0, 0)] = inp.tile([P, 2, 1024], U8, name="wb8_0_0", align_bytes=256)
         for jj in range(2):
             nc.sync.dma_start(out=wb8[(0, 0)][:, jj:jj + 1, :], in_=w2v[:, CYC[0][0][0] * 8 + 2 * CYC[0][0][1] + jj:CYC[0][0][0] * 8 + 2 * CYC[0][0][1] + jj + 1, :])
             if jj == 0:
@@ -396,7 +396,7 @@ def tile_painnmixing_pb_kernel(tc, h, mu_W, mu_VW, q, mu, W2_bytes, W2_scale, b2
         scale_out(0, 3)
         cast(1, 2)
         cast(1, 3)
-        dummy(2)
+        dummy(1)
         quant(0)
         h_quant()
         bias_prep()
@@ -418,7 +418,10 @@ def tile_painnmixing_pb_kernel(tc, h, mu_W, mu_VW, q, mu, W2_bytes, W2_scale, b2
             flush(1)
             if c == -1:
                 t1(1, 0)
+                g_scale(1, 0)
             t1(c + 2, 1)
+            if c == -1:
+                dummy(1)
             if ng > 1:
                 scale_out(c + 2, 1)
             if c == 0:
@@ -433,7 +436,7 @@ def tile_painnmixing_pb_kernel(tc, h, mu_W, mu_VW, q, mu, W2_bytes, W2_scale, b2
                 quant(c + 1)
             mmb(c + 1, 0)
             mmb(c + 1, 1)
-            if c != 0:
+            if c > 0:
                 scale_out(c + 2, 0)
             t1(c + 2, 3)
             g_at(c, 1)

@@ -488,16 +488,16 @@ def tile_painnmixing_pb_kernel(tc, h, mu_W, mu_VW, q, mu, W2_bytes, W2_scale, b2
         t2(4, 3, True)
         mmb(5, 0)
         mmb(5, 1)
-        epi(3, 3)
-        flush(1)
         epi(4, 0)
+        epi(4, 2)
         mmb(5, 2)
         mmb(5, 3)
+        epi(3, 3)
+        flush(1)
         epi(4, 1)
         t2(5, 0)
-        epi(4, 2)
-        t2(5, 1)
         epi(4, 3)
+        t2(5, 1)
         t2(5, 2)
         t2(5, 3, True)
         epi(5, 0)

from contextlib import ExitStack

import concourse.mybir as mybir
from concourse.masks import make_identity

FLOPS = 2 * 512 * 3072 * 1024

F32 = mybir.dt.float32
BF16 = mybir.dt.bfloat16
U32 = mybir.dt.uint32
U8 = mybir.dt.uint8
FP8 = mybir.dt.float8_e4m3fn
FP8X4 = mybir.dt.float8_e4m3fn_x4
ALU = mybir.AluOpType
ACT = mybir.ActivationFunctionType

P = 128
CYC = [
    [(2, 0), (2, 1)],
    [(1, 0), (0, 0)],
    [(1, 1), (0, 1)],
    [(1, 2), (1, 3)],
    [(2, 2), (0, 2)],
    [(2, 3), (0, 3)],
]
IN_PSUM = (0, 1)
MANUAL = True
N_G = [0, 0, 0, 0, 0, 0]
G_AT = {}
G_TILES = [(c, i) for c in range(6) for i in range(N_G[c])]


def tile_painnmixing_pb_kernel(tc, h, mu_W, mu_VW, q, mu, W2_bytes, W2_scale, b2, out_0, out_1):
    nc = tc.nc
    n_cyc = len(CYC)

    with ExitStack() as ctx:
        const = ctx.enter_context(tc.tile_pool(name="const", bufs=1))
        inp = ctx.enter_context(tc.tile_pool(name="inp", bufs=1))
        wbf_pool = ctx.enter_context(tc.tile_pool(name="wbfp", bufs=6))
        grp_pool = ctx.enter_context(tc.tile_pool(name="grpp", bufs=3))
        gbf_pool = ctx.enter_context(tc.tile_pool(name="gbfp", bufs=1))
        code_pool = ctx.enter_context(tc.tile_pool(name="codep", bufs=2))
        xb_pool = ctx.enter_context(tc.tile_pool(name="xbp", bufs=6))
        mo_pool = ctx.enter_context(tc.tile_pool(name="mop", bufs=4))
        qo_pool = ctx.enter_context(tc.tile_pool(name="qop", bufs=6))
        tt_pool = ctx.enter_context(tc.tile_pool(name="ttp", bufs=4))
        pw = ctx.enter_context(tc.psum_pool(name="pw", bufs=3))
        pm = ctx.enter_context(tc.psum_pool(name="pm", bufs=2))
        px = ctx.enter_context(tc.psum_pool(name="px", bufs=3))
        if MANUAL:
            ctx.enter_context(tc.manual_schedule())

        warm = const.tile([P, 1], F32, name="warm")
        warm2 = const.tile([P, 1], F32, name="warm2")
        nc.vector.memset(warm[:], 0.0)
        nc.scalar.activation(out=warm2[:], in_=warm[:], func=ACT.Identity)
        zer = const.tile([P, 512], BF16, name="zer")
        nc.vector.memset(zer[:], 0.0)
        s4 = const.tile([P, 2, 4], F32, name="s4")
        bt = const.tile([P, P], BF16, name="bt")
        nc.vector.memset(bt[:], 0.0)
        nc.scalar.dma_start(out=bt[0:24, :], in_=b2.rearrange("(j p) -> j p", p=P))

        ident_f = const.tile([P, P], F32, name="ident_f")
        make_identity(nc, ident_f[:])
        ident_b = const.tile([P, P], BF16, name="ident_b")
        make_identity(nc, ident_b[:])


        def dummy(k):
            for r in range(k):
                dm = pm.tile([P, 512], F32, name="dm", tag="mx")
                nc.tensor.matmul(out=dm[:], lhsT=zer[:, 0:P], rhs=zer[:], start=True, stop=True)

        dummy(5)
        w2v = W2_bytes.rearrange("(n p) k -> p n k", p=P)
        wb8 = {}

        def load_w(c, pr):
            s, i = CYC[c][pr]
            t = inp.tile([P, 2, 1024], U8, name="wb8_%d_%d" % (c, pr), align_bytes=256)
            rt = s * 8 + 2 * i
            nc.sync.dma_start(out=t[:], in_=w2v[:, rt:rt + 2, :])
            wb8[(c, pr)] = t

        h_sb = inp.tile([P, 4, 1024], BF16, name="h_sb", align_bytes=256)
        hv = h.rearrange("(a p) o k -> p a (o k)", p=P)
        muW_sb = inp.tile([P, 4, 3, 1024], BF16, name="muW_sb", align_bytes=256)
        mu_sb = inp.tile([P, 4, 3, 1024], BF16, name="mu_sb", align_bytes=256)
        muVW_sb = inp.tile([P, 4, 1024], BF16, name="muVW_sb", align_bytes=256)
        q_sb = inp.tile([P, 4, 1024], BF16, name="q_sb", align_bytes=256)

        srow = const.tile([P, 1024], F32, name="srow")

        def load_muw(a):
            nc.sync.dma_start(out=muW_sb[:, a], in_=mu_W[a * P:(a + 1) * P])

        def load_mu(a):
            nc.sync.dma_start(out=mu_sb[:, a], in_=mu[a * P:(a + 1) * P])

        wb8[(0, 0)] = inp.tile([P, 2, 1024], U8, name="wb8_0_0", align_bytes=256)
        for jj in range(2):
            nc.sync.dma_start(out=wb8[(0, 0)][:, jj:jj + 1, :], in_=w2v[:, CYC[0][0][0] * 8 + 2 * CYC[0][0][1] + jj:CYC[0][0][0] * 8 + 2 * CYC[0][0][1] + jj + 1, :])
            if jj == 0:
                nc.sync.dma_start(out=s4[:], in_=W2_scale.rearrange("o (g p t) -> p (o g) t", g=2, p=P, t=4))
        load_w(0, 1)
        load_w(1, 0)
        nc.sync.dma_start(out=h_sb[:, 0:1], in_=hv[:, 0:1])
        nc.sync.dma_start(out=h_sb[:, 1:2], in_=hv[:, 1:2])
        nc.sync.dma_start(out=h_sb[:, 2:4], in_=hv[:, 2:4])
        load_w(2, 0)
        load_w(1, 1)
        load_w(3, 0)
        nc.sync.dma_start(out=muVW_sb[:], in_=mu_VW.rearrange("(a p) o f -> p a (o f)", p=P))
        load_w(2, 1)
        load_w(4, 0)
        nc.sync.dma_start(out=q_sb[:], in_=q.rearrange("(a p) o f -> p a (o f)", p=P))
        load_w(3, 1)
        for a in range(4):
            load_muw(a)
        load_mu(0)
        load_mu(1)
        load_w(4, 1)
        load_mu(2)
        load_mu(3)
        load_w(5, 0)
        load_w(5, 1)

        bias = const.tile([P, 24], F32, name="bias")

        def bias_prep():
            pb = pm.tile([P, P], BF16, name="pb", tag="mx")
            nc.tensor.transpose(out=pb[:], in_=bt[:], identity=ident_b[:])
            nc.vector.tensor_copy(out=bias[:], in_=pb[:, 0:24])

        wbf = {}
        gbf = {}
        wt = {}
        grp = {}
        wc = {}
        ws = {}
        xb = {}
        xT = {}
        qo = {}
        tT = {}

        def ok(c):
            return 0 <= c < n_cyc

        def turn(dst, words):
            for g in range(2):
                for u in range(2):
                    nc.tensor.transpose(
                        out=dst[:, u * 256 + g * P:u * 256 + (g + 1) * P],
                        in_=words[:, 256 * g + u:256 * (g + 1):2],
                        identity=ident_f[:],
                    )

        def cast(c, i):
            if not ok(c):
                return
            if (c, i) in G_TILES:
                return
            pr, jj = divmod(i, 2)
            if (c, pr) not in wbf:
                wbf[(c, pr)] = wbf_pool.tile([P, 2048], BF16, name="wbf", tag="wbf")
            nc.scalar.copy(out=wbf[(c, pr)][:, jj * 1024:(jj + 1) * 1024], in_=wb8[(c, pr)][:, jj, :].bitcast(FP8))

        def vcast(c, i):
            pr, jj = divmod(i, 2)
            if (c, pr) not in wbf:
                wbf[(c, pr)] = wbf_pool.tile([P, 2048], BF16, name="wbf", tag="wbf")
            nc.vector.tensor_copy(out=wbf[(c, pr)][:, jj * 1024:(jj + 1) * 1024], in_=wb8[(c, pr)][:, jj, :].bitcast(FP8))

        def g_scale(c, i):
            pr, jj = divmod(i, 2)
            gbf[(c, i)] = gbf_pool.tile([P, 1024], BF16, name="gbf_%d_%d" % (c, i))
            nc.scalar.copy(out=gbf[(c, i)][:], in_=wb8[(c, pr)][:, jj, :].bitcast(FP8))
            for hf in range(2):
                cs = slice(512 * hf, 512 * (hf + 1))
                nc.gpsimd.tensor_tensor(out=gbf[(c, i)][:, cs], in0=gbf[(c, i)][:, cs], in1=srow[:, cs], op=ALU.mult)

        def t1(c, i):
            if not ok(c):
                return
            pr, jj = divmod(i, 2)
            t = pw.tile([P, 512], F32, name="wt", tag="wt")
            if (c, i) in G_TILES:
                turn(t, gbf[(c, i)][:].bitcast(F32))
            else:
                turn(t, wbf[(c, pr)][:, jj * 1024:(jj + 1) * 1024].bitcast(F32))
            wt[(c, i)] = t

        def scale_out(c, i):
            if not ok(c):
                return
            if c not in grp:
                grp[c] = grp_pool.tile([P, 4096], BF16, name="grp", tag="grp", align_bytes=64)
            if (c, i) in G_TILES:
                nc.scalar.copy(
                    out=grp[c][:, i * 1024:(i + 1) * 1024].bitcast(F32).rearrange("p (x u) -> p x u", u=2),
                    in_=wt[(c, i)][:].rearrange("p (u x) -> p x u", u=2),
                )
                return
            nc.vector.tensor_tensor(
                out=grp[c][:, i * 1024:(i + 1) * 1024].rearrange("p (g r u e) -> p g r u e", g=2, u=2, e=2),
                in0=wt[(c, i)][:].bitcast(BF16).rearrange("p (u g r e) -> p g r u e", u=2, g=2, e=2),
                in1=s4[:].rearrange("p g (u e) -> p g u e", u=2).unsqueeze(2).to_broadcast([P, 2, P, 2, 2]),
                op=ALU.mult,
            )

        def s_scale(c, i, gs):
            if c not in grp:
                grp[c] = grp_pool.tile([P, 4096], BF16, name="grp", tag="grp", align_bytes=64)
            turned = wt[(c, i)][:].bitcast(BF16).rearrange("p (u g r e) -> p u g r e", u=2, g=2, e=2)
            dst = grp[c][:, i * 1024:(i + 1) * 1024].rearrange("p (g r t) -> p g r t", g=2, t=4)
            for g in gs:
                for t in range(4):
                    nc.scalar.activation(out=dst[:, g, :, t], in_=turned[:, t // 2, g, :, t % 2], func=ACT.Copy, scale=s4[:, g, t:t + 1])

        def g_scale(c, i):
            if c not in grp:
                grp[c] = grp_pool.tile([P, 4096], BF16, name="grp", tag="grp", align_bytes=64)
            part = grp[c][:, i * 1024:(i + 1) * 1024]
            nc.scalar.copy(
                out=part.bitcast(F32).rearrange("p (x u) -> p x u", u=2),
                in_=wt[(c, i)][:].rearrange("p (u x) -> p x u", u=2),
            )
            for g in range(2):
                half = part[:, 512 * g:512 * (g + 1)].rearrange("p (r t) -> p r t", t=4)
                nc.gpsimd.tensor_tensor(out=half, in0=half, in1=s4[:, g:g + 1, :].to_broadcast([P, P, 4]), op=ALU.mult)

        def quant(c):
            if not ok(c):
                return
            wc[c] = code_pool.tile([P, 1024], U32, name="wc", tag="wc", align_bytes=64)
            ws[c] = code_pool.tile([P, 1024], U8, name="ws", tag="ws", align_bytes=64)
            nc.vector.quantize_mx(out=wc[c][:].bitcast(FP8X4), scales=ws[c][:], in_=grp[c][:])

        def mmb(c, i):
            if not ok(c):
                return
            pr, jj = divmod(i, 2)
            s, ch = CYC[c][pr]
            acc = pm.tile([P, 512], F32, name="acc", tag="mx")
            for g in range(2):
                c0 = i * 256 + g * P
                nc.tensor.matmul_mx(
                    out=acc[:],
                    lhsT=wc[c][:, c0:c0 + P].bitcast(FP8X4),
                    lhsT_scale=ws[c][:, c0:c0 + P],
                    rhs=hc[:, g * 512:(g + 1) * 512].bitcast(FP8X4),
                    rhs_scale=hs[:, g * 512:(g + 1) * 512],
                    start=(g == 0),
                    stop=(g == 1),
                )
            t = xb_pool.tile([P, 512], F32, name="xb", tag="xb")
            rt = s * 8 + 2 * ch + jj
            nc.scalar.activation(out=t[:], in_=acc[:], func=ACT.Identity, bias=bias[:, rt:rt + 1], scale=1.0)
            xb[(c, i)] = t

        def t2(c, j, in_pw=False):
            if not ok(c):
                return
            pr, hh = divmod(j, 2)
            s, ch = CYC[c][pr]
            if s == 2 and ch in IN_PSUM:
                if hh == 0:
                    t = px.tile([P, 1024], BF16, name="mv", tag="xT")
                    for jj in range(2):
                        for a in range(4):
                            c0 = 256 * ch + jj * P
                            nc.tensor.transpose(out=t[:, jj * 512 + a * P:jj * 512 + (a + 1) * P], in_=muVW_sb[:, a, c0:c0 + P], identity=ident_b[:])
                    xT[(c, j)] = t
                    xT[(c, j + 1)] = t
                return
            if in_pw:
                t = pw.tile([P, 512], F32, name="xT", tag="wt")
            else:
                t = px.tile([P, 512], F32, name="xT", tag="xT")
            more = ch in IN_PSUM
            if s == 0:
                nc.tensor.matmul(
                    out=t[:].rearrange("p (a f) -> p a f", a=2),
                    lhsT=ident_b[:],
                    rhs=q_sb[:, 2 * hh:2 * hh + 2, 256 * ch:256 * (ch + 1)],
                    start=True,
                    stop=False,
                )
            for jj in range(2):
                for a2 in range(2):
                    a = 2 * hh + a2
                    dst = t[:, a2 * 256 + jj * P:a2 * 256 + (jj + 1) * P]
                    src = xb[(c, 2 * pr + jj)][:, a * P:(a + 1) * P]
                    end = jj == 1 and a2 == 1
                    if s == 0:
                        nc.tensor.matmul(out=dst, lhsT=src, rhs=ident_f[:], is_transpose=True, start=False, stop=end and not more)
                        if more:
                            nc.tensor.matmul(out=dst, lhsT=tT[(ch, jj)][:, a * P:(a + 1) * P], rhs=ident_f[:], is_transpose=True, start=False, stop=end)
                    else:
                        nc.tensor.transpose(out=dst, in_=src, identity=ident_f[:])
            xT[(c, j)] = t

        q_out_v = out_0.rearrange("(a p) o f -> p a (o f)", p=P)
        pend = []

        def flush_half():
            mo, a, cs = pend[0]
            nc.sync.dma_start(out=out_1[a * P:(a + 1) * P, :, cs], in_=mo[:, a % 2])
            pend[:1] = []

        def flush(k):
            for r in range(min(2 * k, len(pend))):
                flush_half()

        def epi(c, j):
            if not ok(c):
                return
            pr, hh = divmod(j, 2)
            s, i = CYC[c][pr]
            cs = slice(256 * i, 256 * (i + 1))
            if s == 2 and i in IN_PSUM:
                t = tt_pool.tile([P, 512], F32, name="tT", tag="tT")
                nc.vector.tensor_tensor(out=t[:], in0=xT[(c, j)][:, hh * 512:(hh + 1) * 512], in1=xb[(c, j)][:], op=ALU.mult)
                tT[(i, hh)] = t
                return
            xv = xT[(c, j)][:].rearrange("p (a f) -> p a f", a=2)
            if s == 0 and i in IN_PSUM:
                t = qo_pool.tile([P, 2, 256], F32, name="qo", tag="qo", align_bytes=256)
                nc.scalar.copy(out=t[:], in_=xv)
                nc.sync.dma_start(out=q_out_v[:, 2 * hh:2 * hh + 2, cs], in_=t[:])
                return
            if s == 1:
                mo = mo_pool.tile([P, 2, 3, 256], F32, name="mo", tag="mo", align_bytes=256)
                nc.vector.tensor_tensor(
                    out=mo[:],
                    in0=xv.unsqueeze(2).to_broadcast([P, 2, 3, 256]),
                    in1=muW_sb[:, 2 * hh:2 * hh + 2, :, cs],
                    op=ALU.mult,
                )
                for a2 in range(2):
                    nc.gpsimd.tensor_tensor(out=mo[:, a2], in0=mo[:, a2], in1=mu_sb[:, 2 * hh + a2, :, cs], op=ALU.add)
                pend.extend([(mo, 2 * hh, cs), (mo, 2 * hh + 1, cs)])
            elif s == 2:
                t = qo_pool.tile([P, 2, 256], F32, name="qo", tag="qo", align_bytes=256)
                nc.vector.tensor_tensor(out=t[:], in0=xv, in1=muVW_sb[:, 2 * hh:2 * hh + 2, cs], op=ALU.mult)
                qo[(i, hh)] = t
            else:
                t = qo[(i, hh)]
                nc.vector.tensor_tensor(out=t[:], in0=xv, in1=t[:], op=ALU.add)
                nc.sync.dma_start(out=q_out_v[:, 2 * hh:2 * hh + 2, cs], in_=t[:])

        hgrp = const.tile([P, 4096], BF16, name="hgrp", align_bytes=64)
        hc = const.tile([P, 1024], U32, name="hc", align_bytes=64)
        hs = const.tile([P, 1024], U8, name="hs", align_bytes=64)
        hgw = hgrp[:].bitcast(F32).rearrange("p (g a r u) -> p g a r u", g=2, a=4, r=P, u=2)

        def h_turn(a):
            if a < 3:
                ht = px.tile([P, 512], F32, name="ht", tag="xT")
            else:
                ht = pm.tile([P, 512], F32, name="ht", tag="mx")
            turn(ht, h_sb[:, a, :].bitcast(F32))
            nc.scalar.copy(out=hgw[:, :, a], in_=ht[:].rearrange("p (u g r) -> p g r u", u=2, g=2))

        def h_quant():
            for g in range(2):
                nc.vector.quantize_mx(
                    out=hc[:, g * 512:(g + 1) * 512].bitcast(FP8X4),
                    scales=hs[:, g * 512:(g + 1) * 512],
                    in_=hgrp[:, g * 2048:(g + 1) * 2048],
                )

        vcast(0, 0)
        vcast(0, 1)
        t1(0, 0)
        t1(0, 1)
        dummy(1)
        vcast(0, 2)
        t1(0, 2)
        dummy(1)
        cast(0, 3)
        cast(1, 0)
        cast(1, 1)
        scale_out(0, 0)
        h_turn(0)
        dummy(1)
        scale_out(0, 1)
        t1(0, 3)
        h_turn(1)
        dummy(1)
        scale_out(0, 2)
        h_turn(2)
        h_turn(3)
        scale_out(0, 3)
        cast(1, 2)
        cast(1, 3)
        dummy(1)
        quant(0)
        h_quant()
        bias_prep()
        def a_tile(c, n):
            return N_G[c] + n if ok(c) and N_G[c] + n < 4 else None

        def casts(c, ns):
            for n in ns:
                i = a_tile(c, n)
                if i is not None:
                    cast(c, i)

        def g_at(c, n):
            for ci in G_AT.get((c, n), []):
                g_scale(*ci)

        for c in range(-1, 3):
            ng = N_G[c + 2]
            flush(1)
            if c == -1:
                t1(1, 0)
                g_scale(1, 0)
            t1(c + 2, 1)
            if c == -1:
                dummy(1)
            if ng > 1:
                scale_out(c + 2, 1)
            if c == 0:
                g_scale(2, 0)
            if c >= 0:
                casts(c + 2, [2, 3] if c > 0 else [3])
            g_at(c, 0)
            epi(c, 0)
            t2(c, 3)
            t1(c + 2, 2)
            if c >= 0:
                quant(c + 1)
            mmb(c + 1, 0)
            mmb(c + 1, 1)
            if c > 0:
                scale_out(c + 2, 0)
            t1(c + 2, 3)
            g_at(c, 1)
            epi(c, 1)
            t2(c + 1, 0)
            epi(c, 2)
            t2(c + 1, 1)
            casts(c + 3, [0])
            g_at(c, 2)
            epi(c, 3)
            flush(1)
            mmb(c + 1, 2)
            mmb(c + 1, 3)
            casts(c + 3, [1] if c >= 0 else [1, 2])
            g_at(c, 3)
            if ng < 2:
                scale_out(c + 2, 1)
            t1(c + 3, 0)
            t2(c + 1, 2)
            scale_out(c + 2, 2)
            scale_out(c + 2, 3)
            flush(1)

        flush(1)
        t1(5, 1)
        casts(5, [2, 3])
        s_scale(5, 1, [0])
        epi(3, 0)
        t2(3, 3)
        t1(5, 2)
        quant(4)
        mmb(4, 0)
        mmb(4, 1)
        s_scale(5, 1, [1])
        scale_out(5, 0)
        t1(5, 3)
        epi(3, 1)
        flush(1)
        t2(4, 0)
        mmb(4, 2)
        mmb(4, 3)
        scale_out(5, 2)
        scale_out(5, 3)
        epi(3, 2)
        flush(1)
        t2(4, 1)
        t2(4, 2, True)
        quant(5)
        t2(4, 3, True)
        mmb(5, 0)
        mmb(5, 1)
        epi(4, 0)
        epi(4, 2)
        mmb(5, 2)
        mmb(5, 3)
        epi(3, 3)
        flush(1)
        epi(4, 1)
        t2(5, 0)
        epi(4, 3)
        t2(5, 1)
        t2(5, 2)
        t2(5, 3, True)
        epi(5, 0)
        epi(5, 1)
        flush_half()
        epi(5, 2)
        epi(5, 3)
        flush_half()
